import numpy as np
import ml_dtypes


def mxq(x, axis, fmt="e4m3"):
    dtype, down = {"e4m3": (ml_dtypes.float8_e4m3fn, 7), "e5m2": (ml_dtypes.float8_e5m2, 14)}[fmt]
    v = np.moveaxis(np.asarray(x, np.float32).astype(ml_dtypes.bfloat16).astype(np.float64), axis, -1)
    blocks = v.reshape(v.shape[:-1] + (-1, 32))
    amax = np.abs(blocks).max(-1, keepdims=True)
    byte = np.maximum(np.where(amax > 0, np.frexp(amax)[1] - 1 + 127, 0) - down, 1)
    scale = np.exp2(byte - 127.0)
    codes = (blocks / scale).astype(np.float32).astype(dtype).astype(np.float64)
    return np.moveaxis((codes * scale).reshape(v.shape), -1, axis)


WIDE = False


def mx_kscale(k):
    if not WIDE:
        return np.ones(k)
    levels = np.array([10, -10, 5, -5, 0])
    a = np.random.permutation(np.resize(levels, k // 512 * 4)).reshape(k // 512, 4)
    idx = np.arange(k)
    return np.exp2(a[idx // 512, idx % 128 // 32])


BF16 = ml_dtypes.bfloat16


def bf(x):
    return np.asarray(x, np.float32).astype(BF16)


def f64(x):
    return np.asarray(x).astype(np.float64)


B, D, T, N, H, DH = 2, 512, 1024, 3, 8, 64
EPS = 1e-6
NEG_SLOPE = 0.2


def setup_inputs():
    s = mx_kscale(D)
    return {"x": bf(np.random.standard_normal((B, D, T)) * s[:, None]),
            "qkv": bf(np.random.standard_normal((N, H, D, DH)) * 1.4 / np.sqrt(D) / s[:, None]),
            "norm_w": bf(1.5 + 0.1 * np.random.standard_normal(1))}


def reference(x, qkv, norm_w):
    x = f64(x)
    a = np.where(x >= 0, x, NEG_SLOPE * x)
    aq = mxq(a, 1, "e4m3")
    wq = mxq(f64(qkv), 2, "e4m3")
    y = aq.transpose(0, 2, 1) @ wq.transpose(2, 0, 1, 3).reshape(D, N * H * DH)
    h = y.reshape(B, T, N, H, DH).transpose(2, 0, 3, 1, 4)
    denom = np.mean(h * h, axis=-2, keepdims=True)
    return f64(norm_w) * (h / np.sqrt(denom + EPS))

@@ -1,0 +1,204 @@
+from contextlib import ExitStack
+
+import concourse.mybir as mybir
+from concourse.masks import make_identity
+
+BF16 = mybir.dt.bfloat16
+F32 = mybir.dt.float32
+U32 = mybir.dt.uint32
+U8 = mybir.dt.uint8
+FP8X4 = mybir.dt.float8_e4m3fn_x4
+ALU = mybir.AluOpType
+ACT = mybir.ActivationFunctionType
+AX = mybir.AxisListType
+
+P = 128
+PACK = 4
+BATCH, CHANNELS, SEQ = 2, 512, 1024
+N_QKV, HEADS, HEAD_DIM = 3, 8, 64
+EPS = 1e-6
+NEG_SLOPE = 0.2
+
+BANK = 512
+RUN = SEQ // P
+HALF_RUN = RUN // 2
+GROUP_HEADS = 4
+GROUP_COLS = GROUP_HEADS * HEAD_DIM
+BLOCKS = GROUP_COLS // P
+SEQ_PARTS = SEQ // BANK
+RUNS_PER_BANK = BANK // GROUP_COLS
+STEPS = RUN // RUNS_PER_BANK
+assert STEPS == BLOCKS * SEQ_PARTS
+
+FLOPS = 2 * BATCH * SEQ * CHANNELS * N_QKV * HEADS * HEAD_DIM
+
+
+def tile_mha_pa_kernel(tc, x, qkv, norm_w, out):
+    nc = tc.nc
+    with ExitStack() as ctx:
+        keep = ctx.enter_context(tc.tile_pool(name="keep", bufs=1))
+        stage = ctx.enter_context(tc.tile_pool(name="stage", bufs=2))
+        small = ctx.enter_context(tc.tile_pool(name="small", bufs=3))
+        results = ctx.enter_context(tc.tile_pool(name="results", bufs=4))
+        psum_sums = ctx.enter_context(tc.psum_pool(name="psum_sums", bufs=3))
+        psum_out = ctx.enter_context(tc.psum_pool(name="psum_out", bufs=3))
+        psum_spread = ctx.enter_context(tc.psum_pool(name="psum_spread", bufs=2))
+
+        x_raw = [keep.tile([P, PACK, SEQ], BF16, name="x_raw%d" % b) for b in range(BATCH)]
+        w_raw = [keep.tile([P, HEADS, PACK, HEAD_DIM], BF16, name="w_raw%d" % n) for n in range(N_QKV)]
+
+        def load_x(b):
+            nc.sync.dma_start(out=x_raw[b][:], in_=x[b].rearrange("(p q) t -> p q t", q=PACK))
+
+        def load_w(n):
+            nc.sync.dma_start(out=w_raw[n][:], in_=qkv[n].rearrange("i (p q) j -> p i q j", q=PACK))
+
+        load_x(0)
+        load_w(0)
+        load_w(1)
+        load_w(2)
+        load_x(1)
+
+        eps = keep.tile([P, 1], F32, name="eps")
+        nc.vector.memset(eps[:], EPS)
+        table_warm = keep.tile([P, 1], F32, name="table_warm")
+        nc.scalar.activation(out=table_warm[:], in_=eps[:], func=ACT.Sqrt)
+        gain_bf = keep.tile([P, 1], BF16, name="gain_bf")
+        nc.scalar.dma_start(out=gain_bf[:], in_=norm_w.partition_broadcast(P))
+        gain = keep.tile([P, 1], F32, name="gain")
+        nc.vector.tensor_copy(out=gain[:], in_=gain_bf[:])
+        ident = keep.tile([P, P], F32, name="ident")
+        make_identity(nc, ident[:])
+
+        a_codes = [keep.tile([P, SEQ], U32, name="a_codes%d" % b, align_bytes=64) for b in range(BATCH)]
+        a_scales = [keep.tile([P, SEQ], U8, name="a_scales%d" % b, align_bytes=64) for b in range(BATCH)]
+        w_codes = [keep.tile([P, HEADS * HEAD_DIM], U32, name="w_codes%d" % n, align_bytes=64) for n in range(N_QKV)]
+        w_scales = [keep.tile([P, HEADS * HEAD_DIM], U8, name="w_scales%d" % n, align_bytes=64) for n in range(N_QKV)]
+
+        def prepare_x(b):
+            fifth = stage.tile([P, PACK, SEQ], BF16, name="fifth")
+            nc.vector.tensor_scalar_mul(out=fifth[:], in0=x_raw[b][:], scalar1=NEG_SLOPE)
+            a_grouped = stage.tile([P, RUN, P, PACK], BF16, name="a_grouped", align_bytes=64)
+            x_view = x_raw[b][:].rearrange("p q (m s l) -> p s m q l", s=2, l=HALF_RUN)
+            fifth_view = fifth[:].rearrange("p q (m s l) -> p s m q l", s=2, l=HALF_RUN)
+            a_view = a_grouped[:].rearrange("p (s l) m q -> p s m q l", s=2)
+            for s in range(2):
+                nc.vector.tensor_tensor(out=a_view[:, s], in0=x_view[:, s], in1=fifth_view[:, s], op=ALU.max)
+            for s in range(2):
+                words = slice(s * HALF_RUN * P, (s + 1) * HALF_RUN * P)
+                nc.vector.quantize_mx(
+                    out=a_codes[b][:, words].bitcast(FP8X4),
+                    scales=a_scales[b][:, words],
+                    in_=a_grouped[:, s * HALF_RUN : (s + 1) * HALF_RUN].rearrange("p r m q -> p (r m q)"),
+                )
+
+        def prepare_w(n):
+            w_grouped = stage.tile([P, HEADS, HEAD_DIM, PACK], BF16, name="w_grouped", align_bytes=64)
+            nc.scalar.copy(out=w_grouped[:], in_=w_raw[n][:].rearrange("p i q j -> p i j q"))
+            nc.vector.quantize_mx(
+                out=w_codes[n][:].bitcast(FP8X4),
+                scales=w_scales[n][:],
+                in_=w_grouped[:].rearrange("p i j q -> p (i j q)"),
+            )
+
+        def squares_step(group, sums, k):
+            b, n, first_col = group
+            block, part = divmod(k, SEQ_PARTS)
+            cols = slice(first_col + block * P, first_col + (block + 1) * P)
+            positions = slice(part * BANK, (part + 1) * BANK)
+            h_t = psum_sums.tile([P, BANK], F32, name="h_t")
+            nc.tensor.matmul_mx(
+                out=h_t[:],
+                lhsT=w_codes[n][:, cols].bitcast(FP8X4),
+                lhsT_scale=w_scales[n][:, cols],
+                rhs=a_codes[b][:, positions].bitcast(FP8X4),
+                rhs_scale=a_scales[b][:, positions],
+                start=True,
+                stop=True,
+            )
+            squares = stage.tile([P, BANK], BF16, name="squares")
+            nc.scalar.activation(out=squares[:], in_=h_t[:], func=ACT.Square, accum_out=sums[:, k : k + 1])
+
+        def column_scales(sums):
+            total = small.tile([P, BLOCKS], F32, name="total")
+            nc.vector.tensor_reduce(
+                out=total[:], in_=sums[:].rearrange("p (c s) -> p c s", s=SEQ_PARTS), axis=AX.X, op=ALU.add
+            )
+            rms = small.tile([P, BLOCKS], F32, name="rms")
+            nc.scalar.activation(out=rms[:], in_=total[:], func=ACT.Sqrt, scale=1.0 / SEQ, bias=eps[:, 0:1])
+            inv_rms = small.tile([P, BLOCKS], F32, name="inv_rms")
+            nc.vector.reciprocal(out=inv_rms[:], in_=rms[:])
+            spread = psum_spread.tile([P, GROUP_COLS], F32, name="spread")
+            for c in range(BLOCKS):
+                nc.tensor.transpose(
+                    out=spread[:, c * P : (c + 1) * P],
+                    in_=inv_rms[:, c : c + 1].to_broadcast([P, P]),
+                    identity=ident[:],
+                )
+            scale = small.tile([P, GROUP_COLS], F32, name="scale")
+            nc.scalar.activation(out=scale[:], in_=spread[:], func=ACT.Copy, scale=gain[:, 0:1])
+            return scale
+
+        def result_step(group, scale, result, k):
+            b, n, first_col = group
+            cols = slice(first_col, first_col + GROUP_COLS)
+            h = psum_out.tile([P, RUNS_PER_BANK, GROUP_COLS], F32, name="h")
+            for e in range(RUNS_PER_BANK):
+                r = k * RUNS_PER_BANK + e
+                positions = slice(r * P, (r + 1) * P)
+                nc.tensor.matmul_mx(
+                    out=h[:, e, :],
+                    lhsT=a_codes[b][:, positions].bitcast(FP8X4),
+                    lhsT_scale=a_scales[b][:, positions],
+                    rhs=w_codes[n][:, cols].bitcast(FP8X4),
+                    rhs_scale=w_scales[n][:, cols],
+                    start=True,
+                    stop=True,
+                )
+            nc.vector.tensor_tensor(
+                out=result[:, :, k * RUNS_PER_BANK : (k + 1) * RUNS_PER_BANK, :].rearrange("p i r j -> p r i j"),
+                in0=h[:].rearrange("p r (i j) -> p r i j", j=HEAD_DIM),
+                in1=scale[:]
+                .rearrange("p (i j) -> p i j", j=HEAD_DIM)
+                .unsqueeze(1)
+                .to_broadcast([P, RUNS_PER_BANK, GROUP_HEADS, HEAD_DIM]),
+                op=ALU.mult,
+            )
+
+        def store(group, result):
+            b, n, first_col = group
+            first_head = first_col // HEAD_DIM
+            nc.sync.dma_start(
+                out=out[n, b, first_head : first_head + GROUP_HEADS].rearrange("i (p r) j -> p i (r j)", r=RUN),
+                in_=result[:].rearrange("p i r j -> p i (r j)"),
+            )
+
+        groups = [
+            (b, n, first_col)
+            for b in range(BATCH)
+            for n in range(N_QKV)
+            for first_col in range(0, HEADS * HEAD_DIM, GROUP_COLS)
+        ]
+
+        prepare_w(0)
+        prepare_x(0)
+        sums = small.tile([P, STEPS], F32, name="sums")
+        for k in range(STEPS):
+            squares_step(groups[0], sums, k)
+        scale = column_scales(sums)
+        prepare_w(1)
+        prepare_w(2)
+        prepare_x(1)
+
+        for g, group in enumerate(groups):
+            following = groups[g + 1] if g + 1 < len(groups) else None
+            result = results.tile([P, GROUP_HEADS, RUN, HEAD_DIM], F32, name="result")
+            if following is not None:
+                sums = small.tile([P, STEPS], F32, name="sums")
+            for k in range(STEPS):
+                if following is not None:
+                    squares_step(following, sums, k)
+                result_step(group, scale, result, k)
+            store(group, result)
+            if following is not None:
+                scale = column_scales(sums)

@@ -16,21 +16,23 @@ P = 128
 PACK = 4
 BATCH, CHANNELS, SEQ = 2, 512, 1024
 N_QKV, HEADS, HEAD_DIM = 3, 8, 64
+COLS = HEADS * HEAD_DIM
 EPS = 1e-6
 NEG_SLOPE = 0.2
 
 BANK = 512
 RUN = SEQ // P
 HALF_RUN = RUN // 2
-GROUP_HEADS = 4
-GROUP_COLS = GROUP_HEADS * HEAD_DIM
-BLOCKS = GROUP_COLS // P
+HALF_SEQ = SEQ // 2
+HALF_P = P // 2
+BLOCKS = COLS // P
 SEQ_PARTS = SEQ // BANK
-RUNS_PER_BANK = BANK // GROUP_COLS
-STEPS = RUN // RUNS_PER_BANK
-assert STEPS == BLOCKS * SEQ_PARTS
+STORE_HEADS = 4
+STORE_COLS = STORE_HEADS * HEAD_DIM
+RUNS_PER_BANK = BANK // STORE_COLS
+AHEAD = 2
 
-FLOPS = 2 * BATCH * SEQ * CHANNELS * N_QKV * HEADS * HEAD_DIM
+FLOPS = 2 * BATCH * SEQ * CHANNELS * N_QKV * COLS
 
 
 def tile_mha_pa_kernel(tc, x, qkv, norm_w, out):
@@ -38,26 +40,31 @@ def tile_mha_pa_kernel(tc, x, qkv, norm_w, out):
     with ExitStack() as ctx:
         keep = ctx.enter_context(tc.tile_pool(name="keep", bufs=1))
         stage = ctx.enter_context(tc.tile_pool(name="stage", bufs=2))
-        small = ctx.enter_context(tc.tile_pool(name="small", bufs=3))
+        small = ctx.enter_context(tc.tile_pool(name="small", bufs=AHEAD + 2))
         results = ctx.enter_context(tc.tile_pool(name="results", bufs=4))
         psum_sums = ctx.enter_context(tc.psum_pool(name="psum_sums", bufs=3))
-        psum_out = ctx.enter_context(tc.psum_pool(name="psum_out", bufs=3))
-        psum_spread = ctx.enter_context(tc.psum_pool(name="psum_spread", bufs=2))
+        psum_out = ctx.enter_context(tc.psum_pool(name="psum_out", bufs=4))
+        psum_spread = ctx.enter_context(tc.psum_pool(name="psum_spread", bufs=1))
 
         x_raw = [keep.tile([P, PACK, SEQ], BF16, name="x_raw%d" % b) for b in range(BATCH)]
         w_raw = [keep.tile([P, HEADS, PACK, HEAD_DIM], BF16, name="w_raw%d" % n) for n in range(N_QKV)]
 
-        def load_x(b):
-            nc.sync.dma_start(out=x_raw[b][:], in_=x[b].rearrange("(p q) t -> p q t", q=PACK))
+        def load_x(b, half):
+            positions = slice(half * HALF_SEQ, (half + 1) * HALF_SEQ)
+            nc.sync.dma_start(
+                out=x_raw[b][:, :, positions], in_=x[b, :, positions].rearrange("(p q) t -> p q t", q=PACK)
+            )
 
         def load_w(n):
             nc.sync.dma_start(out=w_raw[n][:], in_=qkv[n].rearrange("i (p q) j -> p i q j", q=PACK))
 
-        load_x(0)
+        load_x(0, 0)
+        load_x(0, 1)
         load_w(0)
         load_w(1)
         load_w(2)
-        load_x(1)
+        load_x(1, 0)
+        load_x(1, 1)
 
         eps = keep.tile([P, 1], F32, name="eps")
         nc.vector.memset(eps[:], EPS)
@@ -72,133 +79,143 @@ def tile_mha_pa_kernel(tc, x, qkv, norm_w, out):
 
         a_codes = [keep.tile([P, SEQ], U32, name="a_codes%d" % b, align_bytes=64) for b in range(BATCH)]
         a_scales = [keep.tile([P, SEQ], U8, name="a_scales%d" % b, align_bytes=64) for b in range(BATCH)]
-        w_codes = [keep.tile([P, HEADS * HEAD_DIM], U32, name="w_codes%d" % n, align_bytes=64) for n in range(N_QKV)]
-        w_scales = [keep.tile([P, HEADS * HEAD_DIM], U8, name="w_scales%d" % n, align_bytes=64) for n in range(N_QKV)]
+        w_codes = [keep.tile([P, COLS], U32, name="w_codes%d" % n, align_bytes=64) for n in range(N_QKV)]
+        w_scales = [keep.tile([P, COLS], U8, name="w_scales%d" % n, align_bytes=64) for n in range(N_QKV)]
 
-        def prepare_x(b):
-            fifth = stage.tile([P, PACK, SEQ], BF16, name="fifth")
-            nc.vector.tensor_scalar_mul(out=fifth[:], in0=x_raw[b][:], scalar1=NEG_SLOPE)
-            a_grouped = stage.tile([P, RUN, P, PACK], BF16, name="a_grouped", align_bytes=64)
+        fifth = [keep.tile([P, PACK, SEQ], BF16, name="fifth%d" % b) for b in range(BATCH)]
+        a_grouped = [keep.tile([P, RUN, P, PACK], BF16, name="a_grouped%d" % b, align_bytes=64) for b in range(BATCH)]
+
+        def prepare_x(b, s):
             x_view = x_raw[b][:].rearrange("p q (m s l) -> p s m q l", s=2, l=HALF_RUN)
-            fifth_view = fifth[:].rearrange("p q (m s l) -> p s m q l", s=2, l=HALF_RUN)
-            a_view = a_grouped[:].rearrange("p (s l) m q -> p s m q l", s=2)
-            for s in range(2):
-                nc.vector.tensor_tensor(out=a_view[:, s], in0=x_view[:, s], in1=fifth_view[:, s], op=ALU.max)
-            for s in range(2):
-                words = slice(s * HALF_RUN * P, (s + 1) * HALF_RUN * P)
-                nc.vector.quantize_mx(
-                    out=a_codes[b][:, words].bitcast(FP8X4),
-                    scales=a_scales[b][:, words],
-                    in_=a_grouped[:, s * HALF_RUN : (s + 1) * HALF_RUN].rearrange("p r m q -> p (r m q)"),
+            fifth_view = fifth[b][:].rearrange("p q (m s l) -> p s m q l", s=2, l=HALF_RUN)
+            a_view = a_grouped[b][:].rearrange("p (s l) m q -> p s m q l", s=2)
+            for half in range(2):
+                if s == 0:
+                    positions = slice(half * HALF_SEQ, (half + 1) * HALF_SEQ)
+                    nc.vector.tensor_scalar_mul(
+                        out=fifth[b][:, :, positions], in0=x_raw[b][:, :, positions], scalar1=NEG_SLOPE
+                    )
+                rows = slice(half * HALF_P, (half + 1) * HALF_P)
+                nc.vector.tensor_tensor(
+                    out=a_view[:, s, rows], in0=x_view[:, s, rows], in1=fifth_view[:, s, rows], op=ALU.max
                 )
+            words = slice(s * HALF_RUN * P, (s + 1) * HALF_RUN * P)
+            nc.vector.quantize_mx(
+                out=a_codes[b][:, words].bitcast(FP8X4),
+                scales=a_scales[b][:, words],
+                in_=a_grouped[b][:, s * HALF_RUN : (s + 1) * HALF_RUN].rearrange("p r m q -> p (r m q)"),
+            )
 
         def prepare_w(n):
             w_grouped = stage.tile([P, HEADS, HEAD_DIM, PACK], BF16, name="w_grouped", align_bytes=64)
-            nc.scalar.copy(out=w_grouped[:], in_=w_raw[n][:].rearrange("p i q j -> p i j q"))
-            nc.vector.quantize_mx(
-                out=w_codes[n][:].bitcast(FP8X4),
-                scales=w_scales[n][:],
-                in_=w_grouped[:].rearrange("p i j q -> p (i j q)"),
-            )
+            for first_head in range(0, HEADS, STORE_HEADS):
+                heads = slice(first_head, first_head + STORE_HEADS)
+                cols = slice(first_head * HEAD_DIM, (first_head + STORE_HEADS) * HEAD_DIM)
+                if n == 0:
+                    nc.scalar.copy(out=w_grouped[:, heads], in_=w_raw[n][:, heads].rearrange("p i q j -> p i j q"))
+                else:
+                    nc.vector.tensor_copy(
+                        out=w_grouped[:, heads].rearrange("p i (c l) q -> p i c q l", l=4),
+                        in_=w_raw[n][:, heads].rearrange("p i q (c l) -> p i c q l", l=4),
+                    )
+                nc.vector.quantize_mx(
+                    out=w_codes[n][:, cols].bitcast(FP8X4),
+                    scales=w_scales[n][:, cols],
+                    in_=w_grouped[:, heads].rearrange("p i j q -> p (i j q)"),
+                )
 
-        def squares_step(group, sums, k):
-            b, n, first_col = group
-            block, part = divmod(k, SEQ_PARTS)
-            cols = slice(first_col + block * P, first_col + (block + 1) * P)
-            positions = slice(part * BANK, (part + 1) * BANK)
-            h_t = psum_sums.tile([P, BANK], F32, name="h_t")
-            nc.tensor.matmul_mx(
-                out=h_t[:],
-                lhsT=w_codes[n][:, cols].bitcast(FP8X4),
-                lhsT_scale=w_scales[n][:, cols],
-                rhs=a_codes[b][:, positions].bitcast(FP8X4),
-                rhs_scale=a_scales[b][:, positions],
-                start=True,
-                stop=True,
-            )
-            squares = stage.tile([P, BANK], BF16, name="squares")
-            nc.scalar.activation(out=squares[:], in_=h_t[:], func=ACT.Square, accum_out=sums[:, k : k + 1])
-
-        def column_scales(sums):
+        def column_scales(b, n, first_block, n_blocks):
+            sums = small.tile([P, SEQ_PARTS, BLOCKS], F32, name="sums")
+            for part in range(SEQ_PARTS):
+                positions = slice(part * BANK, (part + 1) * BANK)
+                for block in range(n_blocks):
+                    cols = slice((first_block + block) * P, (first_block + block + 1) * P)
+                    h_t = psum_sums.tile([P, BANK], F32, name="h_t")
+                    nc.tensor.matmul_mx(
+                        out=h_t[:],
+                        lhsT=w_codes[n][:, cols].bitcast(FP8X4),
+                        lhsT_scale=w_scales[n][:, cols],
+                        rhs=a_codes[b][:, positions].bitcast(FP8X4),
+                        rhs_scale=a_scales[b][:, positions],
+                        start=True,
+                        stop=True,
+                    )
+                    squares = stage.tile([P, BANK], BF16, name="squares")
+                    nc.scalar.activation(
+                        out=squares[:], in_=h_t[:], func=ACT.Square, accum_out=sums[:, part, block : block + 1]
+                    )
             total = small.tile([P, BLOCKS], F32, name="total")
             nc.vector.tensor_reduce(
-                out=total[:], in_=sums[:].rearrange("p (c s) -> p c s", s=SEQ_PARTS), axis=AX.X, op=ALU.add
+                out=total[:, :n_blocks], in_=sums[:, :, :n_blocks].rearrange("p s c -> p c s"), axis=AX.X, op=ALU.add
             )
             rms = small.tile([P, BLOCKS], F32, name="rms")
-            nc.scalar.activation(out=rms[:], in_=total[:], func=ACT.Sqrt, scale=1.0 / SEQ, bias=eps[:, 0:1])
+            nc.scalar.activation(
+                out=rms[:, :n_blocks], in_=total[:, :n_blocks], func=ACT.Sqrt, scale=1.0 / SEQ, bias=eps[:, 0:1]
+            )
             inv_rms = small.tile([P, BLOCKS], F32, name="inv_rms")
-            nc.vector.reciprocal(out=inv_rms[:], in_=rms[:])
-            spread = psum_spread.tile([P, GROUP_COLS], F32, name="spread")
-            for c in range(BLOCKS):
+            nc.vector.reciprocal(out=inv_rms[:, :n_blocks], in_=rms[:, :n_blocks])
+            spread = psum_spread.tile([P, COLS], F32, name="spread")
+            for block in range(n_blocks):
                 nc.tensor.transpose(
-                    out=spread[:, c * P : (c + 1) * P],
-                    in_=inv_rms[:, c : c + 1].to_broadcast([P, P]),
+                    out=spread[:, block * P : (block + 1) * P],
+                    in_=inv_rms[:, block : block + 1].to_broadcast([P, P]),
                     identity=ident[:],
                 )
-            scale = small.tile([P, GROUP_COLS], F32, name="scale")
-            nc.scalar.activation(out=scale[:], in_=spread[:], func=ACT.Copy, scale=gain[:, 0:1])
+            scale = small.tile([P, COLS], F32, name="scale")
+            nc.scalar.activation(
+                out=scale[:, : n_blocks * P], in_=spread[:, : n_blocks * P], func=ACT.Copy, scale=gain[:, 0:1]
+            )
             return scale
 
-        def result_step(group, scale, result, k):
-            b, n, first_col = group
-            cols = slice(first_col, first_col + GROUP_COLS)
-            h = psum_out.tile([P, RUNS_PER_BANK, GROUP_COLS], F32, name="h")
-            for e in range(RUNS_PER_BANK):
-                r = k * RUNS_PER_BANK + e
-                positions = slice(r * P, (r + 1) * P)
-                nc.tensor.matmul_mx(
-                    out=h[:, e, :],
-                    lhsT=a_codes[b][:, positions].bitcast(FP8X4),
-                    lhsT_scale=a_scales[b][:, positions],
-                    rhs=w_codes[n][:, cols].bitcast(FP8X4),
-                    rhs_scale=w_scales[n][:, cols],
-                    start=True,
-                    stop=True,
+        def results_of(b, n, first_block, n_blocks, scale):
+            for first_col in range(first_block * P, (first_block + n_blocks) * P, STORE_COLS):
+                first_head = first_col // HEAD_DIM
+                cols = slice(first_col, first_col + STORE_COLS)
+                scale_cols = slice(first_col - first_block * P, first_col - first_block * P + STORE_COLS)
+                result = results.tile([P, STORE_HEADS, RUN, HEAD_DIM], F32, name="result")
+                for first_run in range(0, RUN, RUNS_PER_BANK):
+                    h = psum_out.tile([P, RUNS_PER_BANK, STORE_COLS], F32, name="h")
+                    for e in range(RUNS_PER_BANK):
+                        positions = slice((first_run + e) * P, (first_run + e + 1) * P)
+                        nc.tensor.matmul_mx(
+                            out=h[:, e, :],
+                            lhsT=a_codes[b][:, positions].bitcast(FP8X4),
+                            lhsT_scale=a_scales[b][:, positions],
+                            rhs=w_codes[n][:, cols].bitcast(FP8X4),
+                            rhs_scale=w_scales[n][:, cols],
+                            start=True,
+                            stop=True,
+                        )
+                    nc.vector.tensor_tensor(
+                        out=result[:, :, first_run : first_run + RUNS_PER_BANK, :].rearrange("p i r j -> p r i j"),
+                        in0=h[:].rearrange("p r (i j) -> p r i j", j=HEAD_DIM),
+                        in1=scale[:, scale_cols]
+                        .rearrange("p (i j) -> p i j", j=HEAD_DIM)
+                        .unsqueeze(1)
+                        .to_broadcast([P, RUNS_PER_BANK, STORE_HEADS, HEAD_DIM]),
+                        op=ALU.mult,
+                    )
+                nc.sync.dma_start(
+                    out=out[n, b, first_head : first_head + STORE_HEADS].rearrange("i (p r) j -> p i (r j)", r=RUN),
+                    in_=result[:].rearrange("p i r j -> p i (r j)"),
                 )
-            nc.vector.tensor_tensor(
-                out=result[:, :, k * RUNS_PER_BANK : (k + 1) * RUNS_PER_BANK, :].rearrange("p i r j -> p r i j"),
-                in0=h[:].rearrange("p r (i j) -> p r i j", j=HEAD_DIM),
-                in1=scale[:]
-                .rearrange("p (i j) -> p i j", j=HEAD_DIM)
-                .unsqueeze(1)
-                .to_broadcast([P, RUNS_PER_BANK, GROUP_HEADS, HEAD_DIM]),
-                op=ALU.mult,
-            )
 
-        def store(group, result):
-            b, n, first_col = group
-            first_head = first_col // HEAD_DIM
-            nc.sync.dma_start(
-                out=out[n, b, first_head : first_head + GROUP_HEADS].rearrange("i (p r) j -> p i (r j)", r=RUN),
-                in_=result[:].rearrange("p i r j -> p i (r j)"),
-            )
+        units = [(b, n, 0, BLOCKS) for b in range(BATCH) for n in range(N_QKV)]
+        b, n, first_block, n_blocks = units.pop()
+        units.append((b, n, 0, BLOCKS // 2))
+        units.append((b, n, BLOCKS // 2, BLOCKS // 2))
+        scales = []
 
-        groups = [
-            (b, n, first_col)
-            for b in range(BATCH)
-            for n in range(N_QKV)
-            for first_col in range(0, HEADS * HEAD_DIM, GROUP_COLS)
-        ]
-
+        prepare_x(0, 0)
         prepare_w(0)
-        prepare_x(0)
-        sums = small.tile([P, STEPS], F32, name="sums")
-        for k in range(STEPS):
-            squares_step(groups[0], sums, k)
-        scale = column_scales(sums)
+        prepare_x(0, 1)
+        scales.append(column_scales(*units[0]))
         prepare_w(1)
+        scales.append(column_scales(*units[1]))
         prepare_w(2)
-        prepare_x(1)
-
-        for g, group in enumerate(groups):
-            following = groups[g + 1] if g + 1 < len(groups) else None
-            result = results.tile([P, GROUP_HEADS, RUN, HEAD_DIM], F32, name="result")
-            if following is not None:
-                sums = small.tile([P, STEPS], F32, name="sums")
-            for k in range(STEPS):
-                if following is not None:
-                    squares_step(following, sums, k)
-                result_step(group, scale, result, k)
-            store(group, result)
-            if following is not None:
-                scale = column_scales(sums)
+        prepare_x(1, 0)
+        prepare_x(1, 1)
+        for u, unit in enumerate(units):
+            if u + AHEAD < len(units):
+                scales.append(column_scales(*units[u + AHEAD]))
+            results_of(*unit, scales[u])

@@ -212,10 +212,12 @@ def tile_mha_pa_kernel(tc, x, qkv, norm_w, out):
         scales.append(column_scales(*units[0]))
         prepare_w(1)
         scales.append(column_scales(*units[1]))
-        prepare_w(2)
-        prepare_x(1, 0)
-        prepare_x(1, 1)
         for u, unit in enumerate(units):
+            if u == 0:
+                prepare_w(2)
+            if u == 1:
+                prepare_x(1, 0)
+                prepare_x(1, 1)
             if u + AHEAD < len(units):
                 scales.append(column_scales(*units[u + AHEAD]))
             results_of(*unit, scales[u])

@@ -27,7 +27,7 @@ HALF_SEQ = SEQ // 2
 HALF_P = P // 2
 BLOCKS = COLS // P
 SEQ_PARTS = SEQ // BANK
-STORE_HEADS = 4
+STORE_HEADS = 2
 STORE_COLS = STORE_HEADS * HEAD_DIM
 RUNS_PER_BANK = BANK // STORE_COLS
 AHEAD = 2
@@ -41,7 +41,7 @@ def tile_mha_pa_kernel(tc, x, qkv, norm_w, out):
         keep = ctx.enter_context(tc.tile_pool(name="keep", bufs=1))
         stage = ctx.enter_context(tc.tile_pool(name="stage", bufs=2))
         small = ctx.enter_context(tc.tile_pool(name="small", bufs=AHEAD + 2))
-        results = ctx.enter_context(tc.tile_pool(name="results", bufs=4))
+        results = ctx.enter_context(tc.tile_pool(name="results", bufs=6))
         psum_sums = ctx.enter_context(tc.psum_pool(name="psum_sums", bufs=3))
         psum_out = ctx.enter_context(tc.psum_pool(name="psum_out", bufs=4))
         psum_spread = ctx.enter_context(tc.psum_pool(name="psum_spread", bufs=1))
@@ -108,9 +108,9 @@ def tile_mha_pa_kernel(tc, x, qkv, norm_w, out):
 
         def prepare_w(n):
             w_grouped = stage.tile([P, HEADS, HEAD_DIM, PACK], BF16, name="w_grouped", align_bytes=64)
-            for first_head in range(0, HEADS, STORE_HEADS):
-                heads = slice(first_head, first_head + STORE_HEADS)
-                cols = slice(first_head * HEAD_DIM, (first_head + STORE_HEADS) * HEAD_DIM)
+            for first_head in range(0, HEADS, HEADS // 2):
+                heads = slice(first_head, first_head + HEADS // 2)
+                cols = slice(first_head * HEAD_DIM, (first_head + HEADS // 2) * HEAD_DIM)
                 if n == 0:
                     nc.scalar.copy(out=w_grouped[:, heads], in_=w_raw[n][:, heads].rearrange("p i q j -> p i j q"))
                 else:
@@ -202,8 +202,9 @@ def tile_mha_pa_kernel(tc, x, qkv, norm_w, out):
 
         units = [(b, n, 0, BLOCKS) for b in range(BATCH) for n in range(N_QKV)]
         b, n, first_block, n_blocks = units.pop()
-        units.append((b, n, 0, BLOCKS // 2))
-        units.append((b, n, BLOCKS // 2, BLOCKS // 2))
+        units.append((b, n, 0, 2))
+        units.append((b, n, 2, 1))
+        units.append((b, n, 3, 1))
         scales = []
 
         prepare_x(0, 0)

@@ -71,11 +71,11 @@ def tile_mha_pa_kernel(tc, x, qkv, norm_w, out):
         table_warm = keep.tile([P, 1], F32, name="table_warm")
         nc.scalar.activation(out=table_warm[:], in_=eps[:], func=ACT.Sqrt)
         gain_bf = keep.tile([P, 1], BF16, name="gain_bf")
-        nc.scalar.dma_start(out=gain_bf[:], in_=norm_w.partition_broadcast(P))
-        gain = keep.tile([P, 1], F32, name="gain")
-        nc.vector.tensor_copy(out=gain[:], in_=gain_bf[:])
+        nc.sync.dma_start(out=gain_bf[:], in_=norm_w.partition_broadcast(P))
         ident = keep.tile([P, P], F32, name="ident")
         make_identity(nc, ident[:])
+        gain = keep.tile([P, 1], F32, name="gain")
+        nc.gpsimd.tensor_copy(out=gain[:], in_=gain_bf[:])
 
         a_codes = [keep.tile([P, SEQ], U32, name="a_codes%d" % b, align_bytes=64) for b in range(BATCH)]
         a_scales = [keep.tile([P, SEQ], U8, name="a_scales%d" % b, align_bytes=64) for b in range(BATCH)]

@@ -69,7 +69,7 @@ def tile_mha_pa_kernel(tc, x, qkv, norm_w, out):
         eps = keep.tile([P, 1], F32, name="eps")
         nc.vector.memset(eps[:], EPS)
         table_warm = keep.tile([P, 1], F32, name="table_warm")
-        nc.scalar.activation(out=table_warm[:], in_=eps[:], func=ACT.Sqrt)
+        nc.scalar.activation(out=table_warm[:], in_=eps[:], func=ACT.Abs_reciprocal_sqrt)
         gain_bf = keep.tile([P, 1], BF16, name="gain_bf")
         nc.sync.dma_start(out=gain_bf[:], in_=norm_w.partition_broadcast(P))
         ident = keep.tile([P, P], F32, name="ident")
@@ -148,12 +148,14 @@ def tile_mha_pa_kernel(tc, x, qkv, norm_w, out):
             nc.vector.tensor_reduce(
                 out=total[:, :n_blocks], in_=sums[:, :, :n_blocks].rearrange("p s c -> p c s"), axis=AX.X, op=ALU.add
             )
-            rms = small.tile([P, BLOCKS], F32, name="rms")
-            nc.scalar.activation(
-                out=rms[:, :n_blocks], in_=total[:, :n_blocks], func=ACT.Sqrt, scale=1.0 / SEQ, bias=eps[:, 0:1]
-            )
             inv_rms = small.tile([P, BLOCKS], F32, name="inv_rms")
-            nc.vector.reciprocal(out=inv_rms[:, :n_blocks], in_=rms[:, :n_blocks])
+            nc.scalar.activation(
+                out=inv_rms[:, :n_blocks],
+                in_=total[:, :n_blocks],
+                func=ACT.Abs_reciprocal_sqrt,
+                scale=1.0 / SEQ,
+                bias=eps[:, 0:1],
+            )
             spread = psum_spread.tile([P, COLS], F32, name="spread")
             for block in range(n_blocks):
                 nc.tensor.transpose(

@@ -31,6 +31,7 @@ STORE_HEADS = 2
 STORE_COLS = STORE_HEADS * HEAD_DIM
 RUNS_PER_BANK = BANK // STORE_COLS
 AHEAD = 2
+WARM_PASSES = 6
 
 FLOPS = 2 * BATCH * SEQ * CHANNELS * N_QKV * COLS
 
@@ -209,6 +210,11 @@ def tile_mha_pa_kernel(tc, x, qkv, norm_w, out):
         units.append((b, n, 3, 1))
         scales = []
 
+        warm = psum_spread.tile([P, COLS], F32, name="spread")
+        for k in range(WARM_PASSES):
+            nc.tensor.matmul(
+                out=warm[:], lhsT=x_raw[0][:, k % PACK, 0:P], rhs=x_raw[0][:, k % PACK, HALF_SEQ:SEQ], start=True, stop=True
+            )
         prepare_x(0, 0)
         prepare_w(0)
         prepare_x(0, 1)

@@ -21,212 +21,288 @@ EPS = 1e-6
 NEG_SLOPE = 0.2
 
 BANK = 512
+PARTS = SEQ // BANK
 RUN = SEQ // P
-HALF_RUN = RUN // 2
+RUN_PART = RUN // PARTS
 HALF_SEQ = SEQ // 2
 HALF_P = P // 2
-BLOCKS = COLS // P
-SEQ_PARTS = SEQ // BANK
-STORE_HEADS = 2
-STORE_COLS = STORE_HEADS * HEAD_DIM
-RUNS_PER_BANK = BANK // STORE_COLS
-AHEAD = 2
-WARM_PASSES = 6
+BLOCK_HEADS = P // HEAD_DIM
+UNIT_BLOCKS = 2
+UNIT_HEADS = UNIT_BLOCKS * BLOCK_HEADS
+UNIT_BANKS = UNIT_BLOCKS * PARTS
+RUNS_PER_BANK = BANK // P
+REGROUP_HEADS = BANK // (PACK * HEAD_DIM)
 
 FLOPS = 2 * BATCH * SEQ * CHANNELS * N_QKV * COLS
 
 
 def tile_mha_pa_kernel(tc, x, qkv, norm_w, out):
     nc = tc.nc
+    units = [
+        (b, n, first_head)
+        for b in range(BATCH)
+        for n in range(N_QKV)
+        for first_head in range(0, HEADS, UNIT_HEADS)
+    ]
+    sum_banks = [(u, part, block) for part in range(PARTS) for u in range(2) for block in range(UNIT_BLOCKS)]
+    sum_banks += [
+        (u, part, block) for u in range(2, len(units)) for part in range(PARTS) for block in range(UNIT_BLOCKS)
+    ]
+    result_banks = [(u, block, half) for u in range(len(units)) for block in range(UNIT_BLOCKS) for half in range(2)]
+
     with ExitStack() as ctx:
         keep = ctx.enter_context(tc.tile_pool(name="keep", bufs=1))
-        stage = ctx.enter_context(tc.tile_pool(name="stage", bufs=2))
-        small = ctx.enter_context(tc.tile_pool(name="small", bufs=AHEAD + 2))
-        results = ctx.enter_context(tc.tile_pool(name="results", bufs=6))
-        psum_sums = ctx.enter_context(tc.psum_pool(name="psum_sums", bufs=3))
-        psum_out = ctx.enter_context(tc.psum_pool(name="psum_out", bufs=4))
-        psum_spread = ctx.enter_context(tc.psum_pool(name="psum_spread", bufs=1))
+        stage = ctx.enter_context(tc.tile_pool(name="stage", bufs=3))
+        small = ctx.enter_context(tc.tile_pool(name="small", bufs=len(units)))
+        results = ctx.enter_context(tc.tile_pool(name="results", bufs=len(units) * UNIT_BLOCKS))
+        psum_scalar = ctx.enter_context(tc.psum_pool(name="psum_scalar", bufs=4))
+        psum_vector = ctx.enter_context(tc.psum_pool(name="psum_vector", bufs=4))
+        ctx.enter_context(tc.manual_schedule())
 
         x_raw = [keep.tile([P, PACK, SEQ], BF16, name="x_raw%d" % b) for b in range(BATCH)]
         w_raw = [keep.tile([P, HEADS, PACK, HEAD_DIM], BF16, name="w_raw%d" % n) for n in range(N_QKV)]
+        gain_bf = keep.tile([P, 1], BF16, name="gain_bf")
 
-        def load_x(b, half):
-            positions = slice(half * HALF_SEQ, (half + 1) * HALF_SEQ)
-            nc.sync.dma_start(
-                out=x_raw[b][:, :, positions], in_=x[b, :, positions].rearrange("(p q) t -> p q t", q=PACK)
-            )
+        def load_x(b):
+            for first in range(0, SEQ, HALF_SEQ):
+                positions = slice(first, first + HALF_SEQ)
+                nc.sync.dma_start(
+                    out=x_raw[b][:, :, positions], in_=x[b, :, positions].rearrange("(p q) t -> p q t", q=PACK)
+                )
 
         def load_w(n):
             nc.sync.dma_start(out=w_raw[n][:], in_=qkv[n].rearrange("i (p q) j -> p i q j", q=PACK))
 
-        load_x(0, 0)
-        load_x(0, 1)
+        load_x(0)
         load_w(0)
         load_w(1)
+        load_x(1)
         load_w(2)
-        load_x(1, 0)
-        load_x(1, 1)
+        nc.sync.dma_start(out=gain_bf[:], in_=norm_w.partition_broadcast(P))
 
         eps = keep.tile([P, 1], F32, name="eps")
         nc.vector.memset(eps[:], EPS)
-        table_warm = keep.tile([P, 1], F32, name="table_warm")
-        nc.scalar.activation(out=table_warm[:], in_=eps[:], func=ACT.Abs_reciprocal_sqrt)
-        gain_bf = keep.tile([P, 1], BF16, name="gain_bf")
-        nc.sync.dma_start(out=gain_bf[:], in_=norm_w.partition_broadcast(P))
+        table_load = keep.tile([P, 1], F32, name="table_load")
+        nc.scalar.activation(out=table_load[:], in_=eps[:], func=ACT.Abs_reciprocal_sqrt)
+        ident_bf = keep.tile([P, P], BF16, name="ident_bf")
+        make_identity(nc, ident_bf[:])
         ident = keep.tile([P, P], F32, name="ident")
         make_identity(nc, ident[:])
         gain = keep.tile([P, 1], F32, name="gain")
         nc.gpsimd.tensor_copy(out=gain[:], in_=gain_bf[:])
 
+        fifth = [keep.tile([P, PACK, SEQ], BF16, name="fifth%d" % b) for b in range(BATCH)]
+        a_grouped = [keep.tile([P, RUN, P, PACK], BF16, name="a_grouped%d" % b, align_bytes=64) for b in range(BATCH)]
+        w_grouped = [
+            keep.tile([P, HEADS, HEAD_DIM, PACK], BF16, name="w_grouped%d" % n, align_bytes=64) for n in range(N_QKV)
+        ]
         a_codes = [keep.tile([P, SEQ], U32, name="a_codes%d" % b, align_bytes=64) for b in range(BATCH)]
         a_scales = [keep.tile([P, SEQ], U8, name="a_scales%d" % b, align_bytes=64) for b in range(BATCH)]
         w_codes = [keep.tile([P, COLS], U32, name="w_codes%d" % n, align_bytes=64) for n in range(N_QKV)]
         w_scales = [keep.tile([P, COLS], U8, name="w_scales%d" % n, align_bytes=64) for n in range(N_QKV)]
 
-        fifth = [keep.tile([P, PACK, SEQ], BF16, name="fifth%d" % b) for b in range(BATCH)]
-        a_grouped = [keep.tile([P, RUN, P, PACK], BF16, name="a_grouped%d" % b, align_bytes=64) for b in range(BATCH)]
+        def scale_x(b, half):
+            positions = slice(half * HALF_SEQ, (half + 1) * HALF_SEQ)
+            nc.vector.tensor_scalar_mul(out=fifth[b][:, :, positions], in0=x_raw[b][:, :, positions], scalar1=NEG_SLOPE)
 
-        def prepare_x(b, s):
-            x_view = x_raw[b][:].rearrange("p q (m s l) -> p s m q l", s=2, l=HALF_RUN)
-            fifth_view = fifth[b][:].rearrange("p q (m s l) -> p s m q l", s=2, l=HALF_RUN)
-            a_view = a_grouped[b][:].rearrange("p (s l) m q -> p s m q l", s=2)
-            for half in range(2):
-                if s == 0:
-                    positions = slice(half * HALF_SEQ, (half + 1) * HALF_SEQ)
-                    nc.vector.tensor_scalar_mul(
-                        out=fifth[b][:, :, positions], in0=x_raw[b][:, :, positions], scalar1=NEG_SLOPE
-                    )
-                rows = slice(half * HALF_P, (half + 1) * HALF_P)
-                nc.vector.tensor_tensor(
-                    out=a_view[:, s, rows], in0=x_view[:, s, rows], in1=fifth_view[:, s, rows], op=ALU.max
-                )
-            words = slice(s * HALF_RUN * P, (s + 1) * HALF_RUN * P)
+        def max_x(b, part, half):
+            rows = slice(half * HALF_P, (half + 1) * HALF_P)
+            x_view = x_raw[b][:].rearrange("p q (m s l) -> p s m q l", s=PARTS, l=RUN_PART)
+            fifth_view = fifth[b][:].rearrange("p q (m s l) -> p s m q l", s=PARTS, l=RUN_PART)
+            a_view = a_grouped[b][:].rearrange("p (s l) m q -> p s m q l", s=PARTS)
+            nc.vector.tensor_tensor(
+                out=a_view[:, part, rows], in0=x_view[:, part, rows], in1=fifth_view[:, part, rows], op=ALU.max
+            )
+
+        def quantise_x(b, part):
+            words = slice(part * BANK, (part + 1) * BANK)
             nc.vector.quantize_mx(
                 out=a_codes[b][:, words].bitcast(FP8X4),
                 scales=a_scales[b][:, words],
-                in_=a_grouped[b][:, s * HALF_RUN : (s + 1) * HALF_RUN].rearrange("p r m q -> p (r m q)"),
+                in_=a_grouped[b][:, part * RUN_PART : (part + 1) * RUN_PART].rearrange("p r m q -> p (r m q)"),
             )
 
-        def prepare_w(n):
-            w_grouped = stage.tile([P, HEADS, HEAD_DIM, PACK], BF16, name="w_grouped", align_bytes=64)
-            for first_head in range(0, HEADS, HEADS // 2):
-                heads = slice(first_head, first_head + HEADS // 2)
-                cols = slice(first_head * HEAD_DIM, (first_head + HEADS // 2) * HEAD_DIM)
-                if n == 0:
-                    nc.scalar.copy(out=w_grouped[:, heads], in_=w_raw[n][:, heads].rearrange("p i q j -> p i j q"))
-                else:
-                    nc.vector.tensor_copy(
-                        out=w_grouped[:, heads].rearrange("p i (c l) q -> p i c q l", l=4),
-                        in_=w_raw[n][:, heads].rearrange("p i q (c l) -> p i c q l", l=4),
-                    )
-                nc.vector.quantize_mx(
-                    out=w_codes[n][:, cols].bitcast(FP8X4),
-                    scales=w_scales[n][:, cols],
-                    in_=w_grouped[:, heads].rearrange("p i j q -> p (i j q)"),
+        def heads_of(first_head):
+            return slice(first_head, first_head + UNIT_HEADS)
+
+        def regroup_w(n, first_head):
+            nc.scalar.copy(
+                out=w_grouped[n][:, heads_of(first_head)],
+                in_=w_raw[n][:, heads_of(first_head)].rearrange("p i q j -> p i j q"),
+            )
+
+        regrouped = {}
+
+        def regroup_pass(n, first_head):
+            regrouped[n, first_head] = psum_scalar.tile([P, UNIT_HEADS, HEAD_DIM, PACK], BF16, name="for_scalar")
+            for i in range(0, UNIT_HEADS, REGROUP_HEADS):
+                nc.tensor.matmul(
+                    out=regrouped[n, first_head][:, i : i + REGROUP_HEADS].rearrange("p i j q -> p i q j"),
+                    lhsT=ident_bf[:],
+                    rhs=w_raw[n][:, first_head + i : first_head + i + REGROUP_HEADS].rearrange("p i q j -> p (i q j)"),
+                    start=True,
+                    stop=True,
                 )
 
-        def column_scales(b, n, first_block, n_blocks):
-            sums = small.tile([P, SEQ_PARTS, BLOCKS], F32, name="sums")
-            for part in range(SEQ_PARTS):
-                positions = slice(part * BANK, (part + 1) * BANK)
-                for block in range(n_blocks):
-                    cols = slice((first_block + block) * P, (first_block + block + 1) * P)
-                    h_t = psum_sums.tile([P, BANK], F32, name="h_t")
-                    nc.tensor.matmul_mx(
-                        out=h_t[:],
-                        lhsT=w_codes[n][:, cols].bitcast(FP8X4),
-                        lhsT_scale=w_scales[n][:, cols],
-                        rhs=a_codes[b][:, positions].bitcast(FP8X4),
-                        rhs_scale=a_scales[b][:, positions],
-                        start=True,
-                        stop=True,
-                    )
-                    squares = stage.tile([P, BANK], BF16, name="squares")
-                    nc.scalar.activation(
-                        out=squares[:], in_=h_t[:], func=ACT.Square, accum_out=sums[:, part, block : block + 1]
-                    )
-            total = small.tile([P, BLOCKS], F32, name="total")
-            nc.vector.tensor_reduce(
-                out=total[:, :n_blocks], in_=sums[:, :, :n_blocks].rearrange("p s c -> p c s"), axis=AX.X, op=ALU.add
+        def regroup_copy(n, first_head):
+            nc.scalar.copy(out=w_grouped[n][:, heads_of(first_head)], in_=regrouped[n, first_head][:])
+
+        def quantise_w(n, first_head):
+            cols = slice(first_head * HEAD_DIM, (first_head + UNIT_HEADS) * HEAD_DIM)
+            nc.vector.quantize_mx(
+                out=w_codes[n][:, cols].bitcast(FP8X4),
+                scales=w_scales[n][:, cols],
+                in_=w_grouped[n][:, heads_of(first_head)].rearrange("p i j q -> p (i j q)"),
             )
-            inv_rms = small.tile([P, BLOCKS], F32, name="inv_rms")
+
+        sums = [small.tile([P, PARTS, UNIT_BLOCKS], F32, name="sums") for u in range(len(units))]
+        products, totals, inverses, spreads, factors = {}, {}, {}, {}, {}
+
+        def block_cols(u, block):
+            first_col = units[u][2] * HEAD_DIM + block * P
+            return slice(first_col, first_col + P)
+
+        def sum_pass(k):
+            u, part, block = sum_banks[k]
+            b, n, first_head = units[u]
+            positions = slice(part * BANK, (part + 1) * BANK)
+            products[k] = psum_scalar.tile([P, BANK], F32, name="for_scalar")
+            nc.tensor.matmul_mx(
+                out=products[k][:],
+                lhsT=w_codes[n][:, block_cols(u, block)].bitcast(FP8X4),
+                lhsT_scale=w_scales[n][:, block_cols(u, block)],
+                rhs=a_codes[b][:, positions].bitcast(FP8X4),
+                rhs_scale=a_scales[b][:, positions],
+                start=True,
+                stop=True,
+            )
+
+        def square(k):
+            u, part, block = sum_banks[k]
+            squares = stage.tile([P, BANK], BF16, name="squares")
             nc.scalar.activation(
-                out=inv_rms[:, :n_blocks],
-                in_=total[:, :n_blocks],
-                func=ACT.Abs_reciprocal_sqrt,
-                scale=1.0 / SEQ,
-                bias=eps[:, 0:1],
+                out=squares[:], in_=products[k][:], func=ACT.Square, accum_out=sums[u][:, part, block : block + 1]
             )
-            spread = psum_spread.tile([P, COLS], F32, name="spread")
-            for block in range(n_blocks):
+
+        def add_parts(u):
+            totals[u] = small.tile([P, UNIT_BLOCKS], F32, name="total")
+            nc.vector.tensor_reduce(
+                out=totals[u][:], in_=sums[u][:].rearrange("p s c -> p c s"), axis=AX.X, op=ALU.add
+            )
+
+        def invert(u):
+            inverses[u] = small.tile([P, UNIT_BLOCKS], F32, name="inverse")
+            nc.scalar.activation(
+                out=inverses[u][:], in_=totals[u][:], func=ACT.Abs_reciprocal_sqrt, scale=1.0 / SEQ, bias=eps[:, 0:1]
+            )
+
+        def spread(u):
+            spreads[u] = psum_scalar.tile([P, UNIT_BLOCKS * P], F32, name="for_scalar")
+            for block in range(UNIT_BLOCKS):
                 nc.tensor.transpose(
-                    out=spread[:, block * P : (block + 1) * P],
-                    in_=inv_rms[:, block : block + 1].to_broadcast([P, P]),
+                    out=spreads[u][:, block * P : (block + 1) * P],
+                    in_=inverses[u][:, block : block + 1].to_broadcast([P, P]),
                     identity=ident[:],
                 )
-            scale = small.tile([P, COLS], F32, name="scale")
-            nc.scalar.activation(
-                out=scale[:, : n_blocks * P], in_=spread[:, : n_blocks * P], func=ACT.Copy, scale=gain[:, 0:1]
-            )
-            return scale
 
-        def results_of(b, n, first_block, n_blocks, scale):
-            for first_col in range(first_block * P, (first_block + n_blocks) * P, STORE_COLS):
-                first_head = first_col // HEAD_DIM
-                cols = slice(first_col, first_col + STORE_COLS)
-                scale_cols = slice(first_col - first_block * P, first_col - first_block * P + STORE_COLS)
-                result = results.tile([P, STORE_HEADS, RUN, HEAD_DIM], F32, name="result")
-                for first_run in range(0, RUN, RUNS_PER_BANK):
-                    h = psum_out.tile([P, RUNS_PER_BANK, STORE_COLS], F32, name="h")
-                    for e in range(RUNS_PER_BANK):
-                        positions = slice((first_run + e) * P, (first_run + e + 1) * P)
-                        nc.tensor.matmul_mx(
-                            out=h[:, e, :],
-                            lhsT=a_codes[b][:, positions].bitcast(FP8X4),
-                            lhsT_scale=a_scales[b][:, positions],
-                            rhs=w_codes[n][:, cols].bitcast(FP8X4),
-                            rhs_scale=w_scales[n][:, cols],
-                            start=True,
-                            stop=True,
-                        )
-                    nc.vector.tensor_tensor(
-                        out=result[:, :, first_run : first_run + RUNS_PER_BANK, :].rearrange("p i r j -> p r i j"),
-                        in0=h[:].rearrange("p r (i j) -> p r i j", j=HEAD_DIM),
-                        in1=scale[:, scale_cols]
-                        .rearrange("p (i j) -> p i j", j=HEAD_DIM)
-                        .unsqueeze(1)
-                        .to_broadcast([P, RUNS_PER_BANK, STORE_HEADS, HEAD_DIM]),
-                        op=ALU.mult,
-                    )
+        def finish_factors(u):
+            factors[u] = small.tile([P, UNIT_BLOCKS * P], F32, name="factor")
+            nc.scalar.activation(out=factors[u][:], in_=spreads[u][:], func=ACT.Copy, scale=gain[:, 0:1])
+
+        result_products, open_result = {}, {}
+
+        def result_pass(j):
+            u, block, half = result_banks[j]
+            b, n, first_head = units[u]
+            result_products[j] = psum_vector.tile([P, RUNS_PER_BANK, P], F32, name="for_vector")
+            for e in range(RUNS_PER_BANK):
+                first = (half * RUNS_PER_BANK + e) * P
+                nc.tensor.matmul_mx(
+                    out=result_products[j][:, e, :],
+                    lhsT=a_codes[b][:, first : first + P].bitcast(FP8X4),
+                    lhsT_scale=a_scales[b][:, first : first + P],
+                    rhs=w_codes[n][:, block_cols(u, block)].bitcast(FP8X4),
+                    rhs_scale=w_scales[n][:, block_cols(u, block)],
+                    start=True,
+                    stop=True,
+                )
+
+        def multiply(j):
+            u, block, half = result_banks[j]
+            b, n, first_head = units[u]
+            if half == 0:
+                open_result[0] = results.tile([P, BLOCK_HEADS, RUN, HEAD_DIM], F32, name="result")
+            result = open_result[0]
+            runs = slice(half * RUNS_PER_BANK, (half + 1) * RUNS_PER_BANK)
+            nc.vector.tensor_tensor(
+                out=result[:, :, runs, :].rearrange("p i r j -> p r i j"),
+                in0=result_products[j][:].rearrange("p r (i j) -> p r i j", j=HEAD_DIM),
+                in1=factors[u][:, block * P : (block + 1) * P]
+                .rearrange("p (i j) -> p i j", j=HEAD_DIM)
+                .unsqueeze(1)
+                .to_broadcast([P, RUNS_PER_BANK, BLOCK_HEADS, HEAD_DIM]),
+                op=ALU.mult,
+            )
+            if half == 1:
+                heads = slice(first_head + block * BLOCK_HEADS, first_head + (block + 1) * BLOCK_HEADS)
                 nc.sync.dma_start(
-                    out=out[n, b, first_head : first_head + STORE_HEADS].rearrange("i (p r) j -> p i (r j)", r=RUN),
+                    out=out[n, b, heads].rearrange("i (p r) j -> p i (r j)", r=RUN),
                     in_=result[:].rearrange("p i r j -> p i (r j)"),
                 )
 
-        units = [(b, n, 0, BLOCKS) for b in range(BATCH) for n in range(N_QKV)]
-        b, n, first_block, n_blocks = units.pop()
-        units.append((b, n, 0, 2))
-        units.append((b, n, 2, 1))
-        units.append((b, n, 3, 1))
-        scales = []
+        for half in range(2):
+            scale_x(0, half)
+            max_x(0, 0, half)
+        quantise_x(0, 0)
+        for half in range(2):
+            regroup_w(0, half * UNIT_HEADS)
+            quantise_w(0, half * UNIT_HEADS)
+            max_x(0, 1, half)
+        quantise_x(0, 1)
 
-        warm = psum_spread.tile([P, COLS], F32, name="spread")
-        for k in range(WARM_PASSES):
-            nc.tensor.matmul(
-                out=warm[:], lhsT=x_raw[0][:, k % PACK, 0:P], rhs=x_raw[0][:, k % PACK, HALF_SEQ:SEQ], start=True, stop=True
-            )
-        prepare_x(0, 0)
-        prepare_w(0)
-        prepare_x(0, 1)
-        scales.append(column_scales(*units[0]))
-        prepare_w(1)
-        scales.append(column_scales(*units[1]))
-        for u, unit in enumerate(units):
-            if u == 0:
-                prepare_w(2)
-            if u == 1:
-                prepare_x(1, 0)
-                prepare_x(1, 1)
-            if u + AHEAD < len(units):
-                scales.append(column_scales(*units[u + AHEAD]))
-            results_of(*unit, scales[u])
+        turns = {}
+
+        def at(turn, action, *args):
+            turns.setdefault(turn, []).append((action, args))
+
+        scalar_turns = []
+        for k, (u, part, block) in enumerate(sum_banks):
+            ahead = k + UNIT_BANKS + UNIT_BANKS // 2
+            if k % UNIT_BANKS == UNIT_BANKS // 2 and ahead // UNIT_BANKS in range(2, N_QKV * HEADS // UNIT_HEADS):
+                b, n, first_head = units[ahead // UNIT_BANKS]
+                scalar_turns.append((regroup_pass, regroup_copy, (n, first_head)))
+            scalar_turns.append((sum_pass, square, (k,)))
+        turn_of = {(action, args): turn for turn, (feed, action, args) in enumerate(scalar_turns)}
+        last_turn = {u: turn_of[square, (k,)] for k, (u, part, block) in enumerate(sum_banks)}
+        result_turns = []
+        for u, block, half in result_banks:
+            result_turns.append(max([last_turn[u] + 5] + [turn + 1 for turn in result_turns[-1:]]))
+
+        for turn, (feed, action, args) in enumerate(scalar_turns):
+            at(turn, action, *args)
+        for u in range(len(units)):
+            at(last_turn[u] + 1, add_parts, u)
+            at(last_turn[u] + 2, invert, u)
+            at(last_turn[u] + 4, finish_factors, u)
+        for n in range(1, N_QKV):
+            for first_head in range(0, HEADS, UNIT_HEADS):
+                at(turn_of[regroup_copy, (n, first_head)] + 2, quantise_w, n, first_head)
+        for half in range(2):
+            at(2 + half, scale_x, 1, half)
+        for piece in range(PARTS * 2):
+            at(5 + 2 * piece, max_x, 1, piece // 2, piece % 2)
+        first_sum_of_x1 = turn_of[square, (len(sum_banks) // 2,)]
+        for part in range(PARTS):
+            at(first_sum_of_x1 - 8 + 6 * part, quantise_x, 1, part)
+        for j, turn in enumerate(result_turns):
+            at(turn, multiply, j)
+        for turn, (feed, action, args) in enumerate(scalar_turns):
+            at(turn - 2, feed, *args)
+        for j, turn in enumerate(result_turns):
+            at(turn - 3, result_pass, j)
+        for u in range(len(units)):
+            at(last_turn[u] + 2, spread, u)
+
+        for turn in sorted(turns):
+            for action, args in turns[turn]:
+                action(*args)

@@ -32,6 +32,7 @@ UNIT_HEADS = UNIT_BLOCKS * BLOCK_HEADS
 UNIT_BANKS = UNIT_BLOCKS * PARTS
 RUNS_PER_BANK = BANK // P
 REGROUP_HEADS = BANK // (PACK * HEAD_DIM)
+WARM_PASSES = 3
 
 FLOPS = 2 * BATCH * SEQ * CHANNELS * N_QKV * COLS
 
@@ -250,6 +251,15 @@ def tile_mha_pa_kernel(tc, x, qkv, norm_w, out):
                     in_=result[:].rearrange("p i r j -> p i (r j)"),
                 )
 
+        unread = psum_vector.tile([P, BANK], F32, name="for_vector")
+        for k in range(WARM_PASSES):
+            nc.tensor.matmul(
+                out=unread[:],
+                lhsT=x_raw[0][:, k % PACK, 0:P],
+                rhs=x_raw[0][:, k % PACK, HALF_SEQ:SEQ],
+                start=True,
+                stop=True,
+            )
         for half in range(2):
             scale_x(0, half)
             max_x(0, 0, half)
@@ -290,18 +300,18 @@ def tile_mha_pa_kernel(tc, x, qkv, norm_w, out):
         for half in range(2):
             at(2 + half, scale_x, 1, half)
         for piece in range(PARTS * 2):
-            at(5 + 2 * piece, max_x, 1, piece // 2, piece % 2)
+            at(4 + 3 * piece, max_x, 1, piece // 2, piece % 2)
         first_sum_of_x1 = turn_of[square, (len(sum_banks) // 2,)]
         for part in range(PARTS):
             at(first_sum_of_x1 - 8 + 6 * part, quantise_x, 1, part)
         for j, turn in enumerate(result_turns):
             at(turn, multiply, j)
         for turn, (feed, action, args) in enumerate(scalar_turns):
-            at(turn - 2, feed, *args)
-        for j, turn in enumerate(result_turns):
-            at(turn - 3, result_pass, j)
+            at(turn - 3, feed, *args)
         for u in range(len(units)):
             at(last_turn[u] + 2, spread, u)
+        for j, turn in enumerate(result_turns):
+            at(turn - 3, result_pass, j)
 
         for turn in sorted(turns):
             for action, args in turns[turn]:

from contextlib import ExitStack

import concourse.mybir as mybir
from concourse.masks import make_identity

BF16 = mybir.dt.bfloat16
F32 = mybir.dt.float32
U32 = mybir.dt.uint32
U8 = mybir.dt.uint8
FP8X4 = mybir.dt.float8_e4m3fn_x4
ALU = mybir.AluOpType
ACT = mybir.ActivationFunctionType
AX = mybir.AxisListType

P = 128
PACK = 4
BATCH, CHANNELS, SEQ = 2, 512, 1024
N_QKV, HEADS, HEAD_DIM = 3, 8, 64
COLS = HEADS * HEAD_DIM
EPS = 1e-6
NEG_SLOPE = 0.2

BANK = 512
PARTS = SEQ // BANK
RUN = SEQ // P
RUN_PART = RUN // PARTS
HALF_SEQ = SEQ // 2
HALF_P = P // 2
BLOCK_HEADS = P // HEAD_DIM
UNIT_BLOCKS = 2
UNIT_HEADS = UNIT_BLOCKS * BLOCK_HEADS
UNIT_BANKS = UNIT_BLOCKS * PARTS
RUNS_PER_BANK = BANK // P
REGROUP_HEADS = BANK // (PACK * HEAD_DIM)
WARM_PASSES = 3

FLOPS = 2 * BATCH * SEQ * CHANNELS * N_QKV * COLS


def tile_mha_pa_kernel(tc, x, qkv, norm_w, out):
    nc = tc.nc
    units = [
        (b, n, first_head)
        for b in range(BATCH)
        for n in range(N_QKV)
        for first_head in range(0, HEADS, UNIT_HEADS)
    ]
    sum_banks = [(u, part, block) for part in range(PARTS) for u in range(2) for block in range(UNIT_BLOCKS)]
    sum_banks += [
        (u, part, block) for u in range(2, len(units)) for part in range(PARTS) for block in range(UNIT_BLOCKS)
    ]
    result_banks = [(u, block, half) for u in range(len(units)) for block in range(UNIT_BLOCKS) for half in range(2)]

    with ExitStack() as ctx:
        keep = ctx.enter_context(tc.tile_pool(name="keep", bufs=1))
        stage = ctx.enter_context(tc.tile_pool(name="stage", bufs=3))
        small = ctx.enter_context(tc.tile_pool(name="small", bufs=len(units)))
        results = ctx.enter_context(tc.tile_pool(name="results", bufs=len(units) * UNIT_BLOCKS))
        psum_scalar = ctx.enter_context(tc.psum_pool(name="psum_scalar", bufs=4))
        psum_vector = ctx.enter_context(tc.psum_pool(name="psum_vector", bufs=4))
        ctx.enter_context(tc.manual_schedule())

        x_raw = [keep.tile([P, PACK, SEQ], BF16, name="x_raw%d" % b) for b in range(BATCH)]
        w_raw = [keep.tile([P, HEADS, PACK, HEAD_DIM], BF16, name="w_raw%d" % n) for n in range(N_QKV)]
        gain_bf = keep.tile([P, 1], BF16, name="gain_bf")

        def load_x(b):
            for first in range(0, SEQ, HALF_SEQ):
                positions = slice(first, first + HALF_SEQ)
                nc.sync.dma_start(
                    out=x_raw[b][:, :, positions], in_=x[b, :, positions].rearrange("(p q) t -> p q t", q=PACK)
                )

        def load_w(n):
            nc.sync.dma_start(out=w_raw[n][:], in_=qkv[n].rearrange("i (p q) j -> p i q j", q=PACK))

        load_x(0)
        load_w(0)
        load_w(1)
        load_x(1)
        load_w(2)
        nc.sync.dma_start(out=gain_bf[:], in_=norm_w.partition_broadcast(P))

        eps = keep.tile([P, 1], F32, name="eps")
        nc.vector.memset(eps[:], EPS)
        table_load = keep.tile([P, 1], F32, name="table_load")
        nc.scalar.activation(out=table_load[:], in_=eps[:], func=ACT.Abs_reciprocal_sqrt)
        ident_bf = keep.tile([P, P], BF16, name="ident_bf")
        make_identity(nc, ident_bf[:])
        ident = keep.tile([P, P], F32, name="ident")
        make_identity(nc, ident[:])
        gain = keep.tile([P, 1], F32, name="gain")
        nc.gpsimd.tensor_copy(out=gain[:], in_=gain_bf[:])

        fifth = [keep.tile([P, PACK, SEQ], BF16, name="fifth%d" % b) for b in range(BATCH)]
        a_grouped = [keep.tile([P, RUN, P, PACK], BF16, name="a_grouped%d" % b, align_bytes=64) for b in range(BATCH)]
        w_grouped = [
            keep.tile([P, HEADS, HEAD_DIM, PACK], BF16, name="w_grouped%d" % n, align_bytes=64) for n in range(N_QKV)
        ]
        a_codes = [keep.tile([P, SEQ], U32, name="a_codes%d" % b, align_bytes=64) for b in range(BATCH)]
        a_scales = [keep.tile([P, SEQ], U8, name="a_scales%d" % b, align_bytes=64) for b in range(BATCH)]
        w_codes = [keep.tile([P, COLS], U32, name="w_codes%d" % n, align_bytes=64) for n in range(N_QKV)]
        w_scales = [keep.tile([P, COLS], U8, name="w_scales%d" % n, align_bytes=64) for n in range(N_QKV)]

        def scale_x(b, half):
            positions = slice(half * HALF_SEQ, (half + 1) * HALF_SEQ)
            nc.vector.tensor_scalar_mul(out=fifth[b][:, :, positions], in0=x_raw[b][:, :, positions], scalar1=NEG_SLOPE)

        def max_x(b, part, half):
            rows = slice(half * HALF_P, (half + 1) * HALF_P)
            x_view = x_raw[b][:].rearrange("p q (m s l) -> p s m q l", s=PARTS, l=RUN_PART)
            fifth_view = fifth[b][:].rearrange("p q (m s l) -> p s m q l", s=PARTS, l=RUN_PART)
            a_view = a_grouped[b][:].rearrange("p (s l) m q -> p s m q l", s=PARTS)
            nc.vector.tensor_tensor(
                out=a_view[:, part, rows], in0=x_view[:, part, rows], in1=fifth_view[:, part, rows], op=ALU.max
            )

        def quantise_x(b, part):
            words = slice(part * BANK, (part + 1) * BANK)
            nc.vector.quantize_mx(
                out=a_codes[b][:, words].bitcast(FP8X4),
                scales=a_scales[b][:, words],
                in_=a_grouped[b][:, part * RUN_PART : (part + 1) * RUN_PART].rearrange("p r m q -> p (r m q)"),
            )

        def heads_of(first_head):
            return slice(first_head, first_head + UNIT_HEADS)

        def regroup_w(n, first_head):
            nc.scalar.copy(
                out=w_grouped[n][:, heads_of(first_head)],
                in_=w_raw[n][:, heads_of(first_head)].rearrange("p i q j -> p i j q"),
            )

        regrouped = {}

        def regroup_pass(n, first_head):
            regrouped[n, first_head] = psum_scalar.tile([P, UNIT_HEADS, HEAD_DIM, PACK], BF16, name="for_scalar")
            for i in range(0, UNIT_HEADS, REGROUP_HEADS):
                nc.tensor.matmul(
                    out=regrouped[n, first_head][:, i : i + REGROUP_HEADS].rearrange("p i j q -> p i q j"),
                    lhsT=ident_bf[:],
                    rhs=w_raw[n][:, first_head + i : first_head + i + REGROUP_HEADS].rearrange("p i q j -> p (i q j)"),
                    start=True,
                    stop=True,
                )

        def regroup_copy(n, first_head):
            nc.scalar.copy(out=w_grouped[n][:, heads_of(first_head)], in_=regrouped[n, first_head][:])

        def quantise_w(n, first_head):
            cols = slice(first_head * HEAD_DIM, (first_head + UNIT_HEADS) * HEAD_DIM)
            nc.vector.quantize_mx(
                out=w_codes[n][:, cols].bitcast(FP8X4),
                scales=w_scales[n][:, cols],
                in_=w_grouped[n][:, heads_of(first_head)].rearrange("p i j q -> p (i j q)"),
            )

        sums = [small.tile([P, PARTS, UNIT_BLOCKS], F32, name="sums") for u in range(len(units))]
        products, totals, inverses, spreads, factors = {}, {}, {}, {}, {}

        def block_cols(u, block):
            first_col = units[u][2] * HEAD_DIM + block * P
            return slice(first_col, first_col + P)

        def sum_pass(k):
            u, part, block = sum_banks[k]
            b, n, first_head = units[u]
            positions = slice(part * BANK, (part + 1) * BANK)
            products[k] = psum_scalar.tile([P, BANK], F32, name="for_scalar")
            nc.tensor.matmul_mx(
                out=products[k][:],
                lhsT=w_codes[n][:, block_cols(u, block)].bitcast(FP8X4),
                lhsT_scale=w_scales[n][:, block_cols(u, block)],
                rhs=a_codes[b][:, positions].bitcast(FP8X4),
                rhs_scale=a_scales[b][:, positions],
                start=True,
                stop=True,
            )

        def square(k):
            u, part, block = sum_banks[k]
            squares = stage.tile([P, BANK], BF16, name="squares")
            nc.scalar.activation(
                out=squares[:], in_=products[k][:], func=ACT.Square, accum_out=sums[u][:, part, block : block + 1]
            )

        def add_parts(u):
            totals[u] = small.tile([P, UNIT_BLOCKS], F32, name="total")
            nc.vector.tensor_reduce(
                out=totals[u][:], in_=sums[u][:].rearrange("p s c -> p c s"), axis=AX.X, op=ALU.add
            )

        def invert(u):
            inverses[u] = small.tile([P, UNIT_BLOCKS], F32, name="inverse")
            nc.scalar.activation(
                out=inverses[u][:], in_=totals[u][:], func=ACT.Abs_reciprocal_sqrt, scale=1.0 / SEQ, bias=eps[:, 0:1]
            )

        def spread(u):
            spreads[u] = psum_scalar.tile([P, UNIT_BLOCKS * P], F32, name="for_scalar")
            for block in range(UNIT_BLOCKS):
                nc.tensor.transpose(
                    out=spreads[u][:, block * P : (block + 1) * P],
                    in_=inverses[u][:, block : block + 1].to_broadcast([P, P]),
                    identity=ident[:],
                )

        def finish_factors(u):
            factors[u] = small.tile([P, UNIT_BLOCKS * P], F32, name="factor")
            nc.scalar.activation(out=factors[u][:], in_=spreads[u][:], func=ACT.Copy, scale=gain[:, 0:1])

        result_products, open_result = {}, {}

        def result_pass(j):
            u, block, half = result_banks[j]
            b, n, first_head = units[u]
            result_products[j] = psum_vector.tile([P, RUNS_PER_BANK, P], F32, name="for_vector")
            for e in range(RUNS_PER_BANK):
                first = (half * RUNS_PER_BANK + e) * P
                nc.tensor.matmul_mx(
                    out=result_products[j][:, e, :],
                    lhsT=a_codes[b][:, first : first + P].bitcast(FP8X4),
                    lhsT_scale=a_scales[b][:, first : first + P],
                    rhs=w_codes[n][:, block_cols(u, block)].bitcast(FP8X4),
                    rhs_scale=w_scales[n][:, block_cols(u, block)],
                    start=True,
                    stop=True,
                )

        def multiply(j):
            u, block, half = result_banks[j]
            b, n, first_head = units[u]
            if half == 0:
                open_result[0] = results.tile([P, BLOCK_HEADS, RUN, HEAD_DIM], F32, name="result")
            result = open_result[0]
            runs = slice(half * RUNS_PER_BANK, (half + 1) * RUNS_PER_BANK)
            nc.vector.tensor_tensor(
                out=result[:, :, runs, :].rearrange("p i r j -> p r i j"),
                in0=result_products[j][:].rearrange("p r (i j) -> p r i j", j=HEAD_DIM),
                in1=factors[u][:, block * P : (block + 1) * P]
                .rearrange("p (i j) -> p i j", j=HEAD_DIM)
                .unsqueeze(1)
                .to_broadcast([P, RUNS_PER_BANK, BLOCK_HEADS, HEAD_DIM]),
                op=ALU.mult,
            )
            if half == 1:
                heads = slice(first_head + block * BLOCK_HEADS, first_head + (block + 1) * BLOCK_HEADS)
                nc.sync.dma_start(
                    out=out[n, b, heads].rearrange("i (p r) j -> p i (r j)", r=RUN),
                    in_=result[:].rearrange("p i r j -> p i (r j)"),
                )

        unread = psum_vector.tile([P, BANK], F32, name="for_vector")
        for k in range(WARM_PASSES):
            nc.tensor.matmul(
                out=unread[:],
                lhsT=x_raw[0][:, k % PACK, 0:P],
                rhs=x_raw[0][:, k % PACK, HALF_SEQ:SEQ],
                start=True,
                stop=True,
            )
        for half in range(2):
            scale_x(0, half)
            max_x(0, 0, half)
        quantise_x(0, 0)
        for half in range(2):
            regroup_w(0, half * UNIT_HEADS)
            quantise_w(0, half * UNIT_HEADS)
            max_x(0, 1, half)
        quantise_x(0, 1)

        turns = {}

        def at(turn, action, *args):
            turns.setdefault(turn, []).append((action, args))

        scalar_turns = []
        for k, (u, part, block) in enumerate(sum_banks):
            ahead = k + UNIT_BANKS + UNIT_BANKS // 2
            if k % UNIT_BANKS == UNIT_BANKS // 2 and ahead // UNIT_BANKS in range(2, N_QKV * HEADS // UNIT_HEADS):
                b, n, first_head = units[ahead // UNIT_BANKS]
                scalar_turns.append((regroup_pass, regroup_copy, (n, first_head)))
            scalar_turns.append((sum_pass, square, (k,)))
        turn_of = {(action, args): turn for turn, (feed, action, args) in enumerate(scalar_turns)}
        last_turn = {u: turn_of[square, (k,)] for k, (u, part, block) in enumerate(sum_banks)}
        result_turns = []
        for u, block, half in result_banks:
            result_turns.append(max([last_turn[u] + 5] + [turn + 1 for turn in result_turns[-1:]]))

        for turn, (feed, action, args) in enumerate(scalar_turns):
            at(turn, action, *args)
        for u in range(len(units)):
            at(last_turn[u] + 1, add_parts, u)
            at(last_turn[u] + 2, invert, u)
            at(last_turn[u] + 4, finish_factors, u)
        for n in range(1, N_QKV):
            for first_head in range(0, HEADS, UNIT_HEADS):
                at(turn_of[regroup_copy, (n, first_head)] + 2, quantise_w, n, first_head)
        for half in range(2):
            at(2 + half, scale_x, 1, half)
        for piece in range(PARTS * 2):
            at(4 + 3 * piece, max_x, 1, piece // 2, piece % 2)
        first_sum_of_x1 = turn_of[square, (len(sum_banks) // 2,)]
        for part in range(PARTS):
            at(first_sum_of_x1 - 8 + 6 * part, quantise_x, 1, part)
        for j, turn in enumerate(result_turns):
            at(turn, multiply, j)
        for turn, (feed, action, args) in enumerate(scalar_turns):
            at(turn - 3, feed, *args)
        for u in range(len(units)):
            at(last_turn[u] + 2, spread, u)
        for j, turn in enumerate(result_turns):
            at(turn - 3, result_pass, j)

        for turn in sorted(turns):
            for action, args in turns[turn]:
                action(*args)
